import numpy as np
import ml_dtypes


def mxq(x, axis, fmt="e4m3"):
    dtype, down = {"e4m3": (ml_dtypes.float8_e4m3fn, 7), "e5m2": (ml_dtypes.float8_e5m2, 14)}[fmt]
    v = np.moveaxis(np.asarray(x, np.float32).astype(ml_dtypes.bfloat16).astype(np.float64), axis, -1)
    blocks = v.reshape(v.shape[:-1] + (-1, 32))
    amax = np.abs(blocks).max(-1, keepdims=True)
    byte = np.maximum(np.where(amax > 0, np.frexp(amax)[1] - 1 + 127, 0) - down, 1)
    scale = np.exp2(byte - 127.0)
    codes = (blocks / scale).astype(np.float32).astype(dtype).astype(np.float64)
    return np.moveaxis((codes * scale).reshape(v.shape), -1, axis)


WIDE = False


def mx_kscale(k):
    if not WIDE:
        return np.ones(k)
    levels = np.array([20, -20, 10, -10, 0])
    a = np.random.permutation(np.resize(levels, k // 512 * 4)).reshape(k // 512, 4)
    idx = np.arange(k)
    return np.exp2(a[idx // 512, idx % 128 // 32])


BF16 = ml_dtypes.bfloat16


def bf(x):
    return np.asarray(x, np.float32).astype(BF16)


def f64(x):
    return np.asarray(x).astype(np.float64)


B, N, AB, MAXN, BB, H = 1, 32, 352, 255, 32, 512
TAIL = AB - (MAXN + 1)
AF = AB + TAIL
FB = AF + BB + BB
T = B * N * N


def gated_features(f_atoms, f_bonds, adj):
    fa = np.concatenate([f_atoms, f_atoms[:, :, MAXN + 1:]], axis=-1)
    fa_exp = np.broadcast_to(fa[:, :, None, :], (B, N, N, AF))
    fb = np.concatenate([fa_exp, f_bonds, f_bonds], axis=-1)
    return adj[..., None] * fb


def setup_inputs():
    s = mx_kscale(T).reshape(B, N, N)
    f_atoms = np.random.standard_normal((B, N, AB))
    f_bonds = np.random.standard_normal((B, N, N, BB))
    adj = np.random.uniform(size=(B, N, N)) * 4.0 / N * s
    W_i_w = np.random.standard_normal((H, FB)) * 0.1 * N / np.sqrt(FB)
    g = np.random.standard_normal((B, N, N, H)) * np.exp2(np.random.randint(-12, 1, (B, N, N, 1))) / s[..., None]
    return {"f_atoms": bf(f_atoms), "f_bonds": bf(f_bonds), "adj": bf(adj), "W_i_w": bf(W_i_w), "grad_out": bf(g)}


def reference(f_atoms, f_bonds, adj, W_i_w, grad_out):
    gf = gated_features(f64(f_atoms), f64(f_bonds), f64(adj)).reshape(T, FB)
    go = f64(grad_out).reshape(T, H)
    return mxq(go, 0, "e5m2").T @ mxq(gf, 0, "e4m3")

@@ -1,0 +1,145 @@
+from contextlib import ExitStack
+
+import concourse.mybir as mybir
+from concourse.masks import make_identity
+
+BF16 = mybir.dt.bfloat16
+F32 = mybir.dt.float32
+I32 = mybir.dt.int32
+U32 = mybir.dt.uint32
+U8 = mybir.dt.uint8
+E4M3_X4 = mybir.dt.float8_e4m3fn_x4
+E5M2_X4 = mybir.dt.float8_e5m2_x4
+
+P = 128
+PACK = 4
+K_PASS = P * PACK
+
+ATOMS = 32
+TOKENS = ATOMS * ATOMS
+PASSES = TOKENS // K_PASS
+ATOMS_PER_PASS = ATOMS // PASSES
+ROWS_PER_ATOM = P // ATOMS_PER_PASS
+
+AB = 352
+REPEATED = 96
+BB = 32
+DISTINCT = AB + BB
+FB = AB + REPEATED + BB + BB
+H = 512
+H_TILES = H // P
+
+FLOPS = 2 * TOKENS * H * FB
+BYTES = 2 * (TOKENS * H + ATOMS * AB + TOKENS * BB + TOKENS) + 4 * H * FB
+
+
+def tile_mpnencoder_pa_s_kernel(tc, f_atoms, f_bonds, adj, W_i_w, grad_out, out):
+    nc = tc.nc
+    with ExitStack() as ctx:
+        keep = ctx.enter_context(tc.tile_pool(name="keep", bufs=1))
+        psum = ctx.enter_context(tc.psum_pool(name="psum", bufs=1))
+        ctx.enter_context(tc.manual_schedule())
+
+        ident = keep.tile([P, P], BF16)
+        spread = keep.tile([P, ATOMS, ROWS_PER_ATOM], BF16)
+        atoms = keep.tile([P, AB], BF16)
+        adj_t = keep.tile([P, PASSES, PACK], BF16)
+        bonds_t = keep.tile([P, PASSES, PACK, BB], BF16)
+        go_raw = keep.tile([P, PASSES, PACK, H], BF16)
+        go_grouped = keep.tile([P, PASSES, H, PACK], BF16, align_bytes=64)
+        go_codes = keep.tile([P, PASSES, H], U32, align_bytes=64)
+        go_scales = keep.tile([P, PASSES, H], U8, align_bytes=64)
+        g_grouped = keep.tile([P, PASSES, DISTINCT, PACK], BF16, align_bytes=64)
+        g_codes = keep.tile([P, PASSES, FB], U32, align_bytes=64)
+        g_scales = keep.tile([P, PASSES, FB], U8, align_bytes=64)
+        result = keep.tile([P, H_TILES, FB], F32)
+
+        go_rows = grad_out.rearrange("b m n h -> (b m n) h").rearrange(
+            "(c p j) h -> c p (j h)", c=PASSES, p=P, j=PACK
+        )
+        nc.sync.dma_start(out=atoms[0:ATOMS, :], in_=f_atoms.rearrange("b m f -> (b m) f"))
+        nc.sync.dma_start(
+            out=adj_t[:],
+            in_=adj.rearrange("b m n -> (b m n)").rearrange("(c p j) -> p c j", c=PASSES, p=P, j=PACK),
+        )
+        nc.sync.dma_start(out=go_raw[:, 0].rearrange("p j h -> p (j h)"), in_=go_rows[0])
+        nc.sync.dma_start(
+            out=bonds_t[:].rearrange("p c j e -> p c (j e)"),
+            in_=f_bonds.rearrange("b m n e -> (b m n) e").rearrange(
+                "(c p j) e -> p c (j e)", c=PASSES, p=P, j=PACK
+            ),
+        )
+        nc.sync.dma_start(out=go_raw[:, 1].rearrange("p j h -> p (j h)"), in_=go_rows[1])
+
+        make_identity(nc, ident[:])
+        nc.vector.memset(atoms[32:64, :], 0.0)
+        nc.vector.memset(atoms[64:128, :], 0.0)
+        nc.vector.tensor_copy(
+            out=spread[:],
+            in_=ident[:, 0:ATOMS].unsqueeze(2).to_broadcast([P, ATOMS, ROWS_PER_ATOM]),
+        )
+        nc.vector.memset(g_codes[:, :, DISTINCT:FB].bitcast(I32), 0)
+        nc.vector.memset(g_scales[:, :, DISTINCT:FB].bitcast(I32), 0)
+
+        atom_rows = [psum.tile([P, AB], F32, name="atom_rows%d" % c) for c in range(PASSES)]
+        for c in range(PASSES):
+            nc.tensor.matmul(
+                out=atom_rows[c][:],
+                lhsT=spread[:, c * ATOMS_PER_PASS : (c + 1) * ATOMS_PER_PASS, :].rearrange("k m r -> k (m r)"),
+                rhs=atoms[:],
+                start=True,
+                stop=True,
+            )
+
+        acc = [psum.tile([P, FB], F32, name="acc%d" % i) for i in range(H_TILES)]
+        for c in range(PASSES):
+            for i in range(H_TILES):
+                cols = slice(i * P, (i + 1) * P)
+                nc.scalar.copy(
+                    out=go_grouped[:, c, cols, :].rearrange("p (u v) j -> p u j v", v=4),
+                    in_=go_raw[:, c, :, cols].rearrange("p j (u v) -> p u j v", v=4),
+                )
+            nc.vector.tensor_tensor(
+                out=g_grouped[:, c, 0:AB, :],
+                in0=atom_rows[c][:].unsqueeze(2).to_broadcast([P, AB, PACK]),
+                in1=adj_t[:, c, :].unsqueeze(1).to_broadcast([P, AB, PACK]),
+                op=mybir.AluOpType.mult,
+            )
+            nc.vector.tensor_tensor(
+                out=g_grouped[:, c, AB:DISTINCT, :],
+                in0=bonds_t[:, c].rearrange("p j e -> p e j"),
+                in1=adj_t[:, c, :].unsqueeze(1).to_broadcast([P, BB, PACK]),
+                op=mybir.AluOpType.mult,
+            )
+            for lo, hi in ((0, 256), (256, DISTINCT)):
+                nc.vector.quantize_mx(
+                    out=g_codes[:, c, lo:hi].bitcast(E4M3_X4),
+                    scales=g_scales[:, c, lo:hi],
+                    in_=g_grouped[:, c, lo:hi, :].rearrange("p f j -> p (f j)"),
+                )
+            for i in range(H_TILES):
+                cols = slice(i * P, (i + 1) * P)
+                nc.vector.quantize_mx(
+                    out=go_codes[:, c, cols].bitcast(E5M2_X4),
+                    scales=go_scales[:, c, cols],
+                    in_=go_grouped[:, c, cols, :].rearrange("p h j -> p (h j)"),
+                )
+                nc.tensor.matmul_mx(
+                    out=acc[i][:],
+                    lhsT=go_codes[:, c, cols].bitcast(E5M2_X4),
+                    lhsT_scale=go_scales[:, c, cols],
+                    rhs=g_codes[:, c, :].bitcast(E4M3_X4),
+                    rhs_scale=g_scales[:, c, :],
+                    start=(c == 0),
+                    stop=(c == PASSES - 1),
+                )
+
+        for i in range(H_TILES):
+            copy = nc.scalar.copy if i % 2 == 0 else nc.vector.tensor_copy
+            copy(out=result[:, i, 0:AB], in_=acc[i][:, 0:AB])
+            copy(out=result[:, i, AB : AB + REPEATED], in_=acc[i][:, AB - REPEATED : AB])
+            copy(
+                out=result[:, i, AB + REPEATED : FB].rearrange("p (r e) -> p r e", r=2),
+                in_=acc[i][:, AB:DISTINCT].unsqueeze(1).to_broadcast([P, 2, BB]),
+            )
+            nc.sync.dma_start(out=out[i * P : (i + 1) * P, :], in_=result[:, i, :])

@@ -81,15 +81,17 @@ def tile_mpnencoder_pa_s_kernel(tc, f_atoms, f_bonds, adj, W_i_w, grad_out, out)
         nc.vector.memset(g_codes[:, :, DISTINCT:FB].bitcast(I32), 0)
         nc.vector.memset(g_scales[:, :, DISTINCT:FB].bitcast(I32), 0)
 
-        atom_rows = [psum.tile([P, AB], F32, name="atom_rows%d" % c) for c in range(PASSES)]
+        atom_rows = [psum.tile([P, AB, 2], BF16, name="atom_rows%d" % c) for c in range(PASSES)]
         for c in range(PASSES):
-            nc.tensor.matmul(
-                out=atom_rows[c][:],
-                lhsT=spread[:, c * ATOMS_PER_PASS : (c + 1) * ATOMS_PER_PASS, :].rearrange("k m r -> k (m r)"),
-                rhs=atoms[:],
-                start=True,
-                stop=True,
-            )
+            for half in range(2):
+                feats = slice(half * (AB // 2), (half + 1) * (AB // 2))
+                nc.tensor.matmul(
+                    out=atom_rows[c][:, feats, :].rearrange("p f e -> p (f e)"),
+                    lhsT=spread[:, c * ATOMS_PER_PASS : (c + 1) * ATOMS_PER_PASS, :].rearrange("k m r -> k (m r)"),
+                    rhs=atoms[:, feats].unsqueeze(2).to_broadcast([P, AB // 2, 2]),
+                    start=True,
+                    stop=True,
+                )
 
         acc = [psum.tile([P, FB], F32, name="acc%d" % i) for i in range(H_TILES)]
         for c in range(PASSES):
@@ -100,9 +102,9 @@ def tile_mpnencoder_pa_s_kernel(tc, f_atoms, f_bonds, adj, W_i_w, grad_out, out)
                     in_=go_raw[:, c, :, cols].rearrange("p j (u v) -> p u j v", v=4),
                 )
             nc.vector.tensor_tensor(
-                out=g_grouped[:, c, 0:AB, :],
-                in0=atom_rows[c][:].unsqueeze(2).to_broadcast([P, AB, PACK]),
-                in1=adj_t[:, c, :].unsqueeze(1).to_broadcast([P, AB, PACK]),
+                out=g_grouped[:, c, 0:AB, :].rearrange("p f (a e) -> p f a e", e=2),
+                in0=atom_rows[c][:].unsqueeze(2).to_broadcast([P, AB, 2, 2]),
+                in1=adj_t[:, c, :].rearrange("p (a e) -> p a e", e=2).unsqueeze(1).to_broadcast([P, AB, 2, 2]),
                 op=mybir.AluOpType.mult,
             )
             nc.vector.tensor_tensor(

@@ -62,14 +62,14 @@ def tile_mpnencoder_pa_s_kernel(tc, f_atoms, f_bonds, adj, W_i_w, grad_out, out)
             out=adj_t[:],
             in_=adj.rearrange("b m n -> (b m n)").rearrange("(c p j) -> p c j", c=PASSES, p=P, j=PACK),
         )
-        nc.sync.dma_start(out=go_raw[:, 0].rearrange("p j h -> p (j h)"), in_=go_rows[0])
         nc.sync.dma_start(
             out=bonds_t[:].rearrange("p c j e -> p c (j e)"),
             in_=f_bonds.rearrange("b m n e -> (b m n) e").rearrange(
                 "(c p j) e -> p c (j e)", c=PASSES, p=P, j=PACK
             ),
         )
-        nc.sync.dma_start(out=go_raw[:, 1].rearrange("p j h -> p (j h)"), in_=go_rows[1])
+        for c in range(PASSES):
+            nc.sync.dma_start(out=go_raw[:, c].rearrange("p j h -> p (j h)"), in_=go_rows[c])
 
         make_identity(nc, ident[:])
         nc.vector.memset(atoms[32:64, :], 0.0)
@@ -80,6 +80,13 @@ def tile_mpnencoder_pa_s_kernel(tc, f_atoms, f_bonds, adj, W_i_w, grad_out, out)
         )
         nc.vector.memset(g_codes[:, :, DISTINCT:FB].bitcast(I32), 0)
         nc.vector.memset(g_scales[:, :, DISTINCT:FB].bitcast(I32), 0)
+
+        nc.gpsimd.tensor_tensor(
+            out=g_grouped[:, :, AB:DISTINCT, :],
+            in0=bonds_t[:].rearrange("p c j e -> p c e j"),
+            in1=adj_t[:].unsqueeze(2).to_broadcast([P, PASSES, BB, PACK]),
+            op=mybir.AluOpType.mult,
+        )
 
         atom_rows = [psum.tile([P, AB, 2], BF16, name="atom_rows%d" % c) for c in range(PASSES)]
         for c in range(PASSES):
@@ -93,26 +100,24 @@ def tile_mpnencoder_pa_s_kernel(tc, f_atoms, f_bonds, adj, W_i_w, grad_out, out)
                     stop=True,
                 )
 
+        def regroup(copy, c, i):
+            cols = slice(i * P, (i + 1) * P)
+            copy(
+                out=go_grouped[:, c, cols, :].rearrange("p (u v) j -> p u j v", v=4),
+                in_=go_raw[:, c, :, cols].rearrange("p j (u v) -> p u j v", v=4),
+            )
+
         acc = [psum.tile([P, FB], F32, name="acc%d" % i) for i in range(H_TILES)]
         for c in range(PASSES):
-            for i in range(H_TILES):
-                cols = slice(i * P, (i + 1) * P)
-                nc.scalar.copy(
-                    out=go_grouped[:, c, cols, :].rearrange("p (u v) j -> p u j v", v=4),
-                    in_=go_raw[:, c, :, cols].rearrange("p j (u v) -> p u j v", v=4),
-                )
+            for i in range(1, H_TILES):
+                regroup(nc.scalar.copy, c, i)
             nc.vector.tensor_tensor(
                 out=g_grouped[:, c, 0:AB, :].rearrange("p f (a e) -> p f a e", e=2),
                 in0=atom_rows[c][:].unsqueeze(2).to_broadcast([P, AB, 2, 2]),
                 in1=adj_t[:, c, :].rearrange("p (a e) -> p a e", e=2).unsqueeze(1).to_broadcast([P, AB, 2, 2]),
                 op=mybir.AluOpType.mult,
             )
-            nc.vector.tensor_tensor(
-                out=g_grouped[:, c, AB:DISTINCT, :],
-                in0=bonds_t[:, c].rearrange("p j e -> p e j"),
-                in1=adj_t[:, c, :].unsqueeze(1).to_broadcast([P, BB, PACK]),
-                op=mybir.AluOpType.mult,
-            )
+            regroup(nc.vector.tensor_copy, c, 0)
             for lo, hi in ((0, 256), (256, DISTINCT)):
                 nc.vector.quantize_mx(
                     out=g_codes[:, c, lo:hi].bitcast(E4M3_X4),

@@ -10,6 +10,8 @@ U32 = mybir.dt.uint32
 U8 = mybir.dt.uint8
 E4M3_X4 = mybir.dt.float8_e4m3fn_x4
 E5M2_X4 = mybir.dt.float8_e5m2_x4
+MULT = mybir.AluOpType.mult
+ADD = mybir.AluOpType.add
 
 P = 128
 PACK = 4
@@ -22,12 +24,14 @@ ATOMS_PER_PASS = ATOMS // PASSES
 ROWS_PER_ATOM = P // ATOMS_PER_PASS
 
 AB = 352
+HALF = AB // 2
 REPEATED = 96
 BB = 32
 DISTINCT = AB + BB
 FB = AB + REPEATED + BB + BB
 H = 512
 H_TILES = H // P
+HELPED = H_TILES - 1
 
 FLOPS = 2 * TOKENS * H * FB
 BYTES = 2 * (TOKENS * H + ATOMS * AB + TOKENS * BB + TOKENS) + 4 * H * FB
@@ -53,10 +57,9 @@ def tile_mpnencoder_pa_s_kernel(tc, f_atoms, f_bonds, adj, W_i_w, grad_out, out)
         g_codes = keep.tile([P, PASSES, FB], U32, align_bytes=64)
         g_scales = keep.tile([P, PASSES, FB], U8, align_bytes=64)
         result = keep.tile([P, H_TILES, FB], F32)
+        atom_rows = [psum.tile([P, AB, 2], BF16, name="atom_rows%d" % c) for c in range(PASSES)]
+        acc = [psum.tile([P, FB], F32, name="acc%d" % i) for i in range(H_TILES)]
 
-        go_rows = grad_out.rearrange("b m n h -> (b m n) h").rearrange(
-            "(c p j) h -> c p (j h)", c=PASSES, p=P, j=PACK
-        )
         nc.sync.dma_start(out=atoms[0:ATOMS, :], in_=f_atoms.rearrange("b m f -> (b m) f"))
         nc.sync.dma_start(
             out=adj_t[:],
@@ -67,6 +70,9 @@ def tile_mpnencoder_pa_s_kernel(tc, f_atoms, f_bonds, adj, W_i_w, grad_out, out)
             in_=f_bonds.rearrange("b m n e -> (b m n) e").rearrange(
                 "(c p j) e -> p c (j e)", c=PASSES, p=P, j=PACK
             ),
+        )
+        go_rows = grad_out.rearrange("b m n h -> (b m n) h").rearrange(
+            "(c p j) h -> c p (j h)", c=PASSES, p=P, j=PACK
         )
         for c in range(PASSES):
             nc.sync.dma_start(out=go_raw[:, c].rearrange("p j h -> p (j h)"), in_=go_rows[c])
@@ -81,65 +87,93 @@ def tile_mpnencoder_pa_s_kernel(tc, f_atoms, f_bonds, adj, W_i_w, grad_out, out)
         nc.vector.memset(g_codes[:, :, DISTINCT:FB].bitcast(I32), 0)
         nc.vector.memset(g_scales[:, :, DISTINCT:FB].bitcast(I32), 0)
 
-        nc.gpsimd.tensor_tensor(
-            out=g_grouped[:, :, AB:DISTINCT, :],
-            in0=bonds_t[:].rearrange("p c j e -> p c e j"),
-            in1=adj_t[:].unsqueeze(2).to_broadcast([P, PASSES, BB, PACK]),
-            op=mybir.AluOpType.mult,
-        )
+        def halves(half):
+            return slice(half * HALF, (half + 1) * HALF)
 
-        atom_rows = [psum.tile([P, AB, 2], BF16, name="atom_rows%d" % c) for c in range(PASSES)]
-        for c in range(PASSES):
-            for half in range(2):
-                feats = slice(half * (AB // 2), (half + 1) * (AB // 2))
-                nc.tensor.matmul(
-                    out=atom_rows[c][:, feats, :].rearrange("p f e -> p (f e)"),
-                    lhsT=spread[:, c * ATOMS_PER_PASS : (c + 1) * ATOMS_PER_PASS, :].rearrange("k m r -> k (m r)"),
-                    rhs=atoms[:, feats].unsqueeze(2).to_broadcast([P, AB // 2, 2]),
-                    start=True,
-                    stop=True,
-                )
+        def spread_atoms(c, half):
+            nc.tensor.matmul(
+                out=atom_rows[c][:, halves(half), :].rearrange("p f e -> p (f e)"),
+                lhsT=spread[:, c * ATOMS_PER_PASS : (c + 1) * ATOMS_PER_PASS, :].rearrange("k m r -> k (m r)"),
+                rhs=atoms[:, halves(half)].unsqueeze(2).to_broadcast([P, HALF, 2]),
+                start=True,
+                stop=True,
+            )
+
+        def gate_atoms(c, half):
+            nc.vector.tensor_tensor(
+                out=g_grouped[:, c, halves(half), :].rearrange("p f (a e) -> p f a e", e=2),
+                in0=atom_rows[c][:, halves(half), :].unsqueeze(2).to_broadcast([P, HALF, 2, 2]),
+                in1=adj_t[:, c, :].rearrange("p (a e) -> p a e", e=2).unsqueeze(1).to_broadcast([P, HALF, 2, 2]),
+                op=MULT,
+            )
+
+        def tile_cols(i):
+            return slice(i * P, (i + 1) * P)
 
         def regroup(copy, c, i):
-            cols = slice(i * P, (i + 1) * P)
             copy(
-                out=go_grouped[:, c, cols, :].rearrange("p (u v) j -> p u j v", v=4),
-                in_=go_raw[:, c, :, cols].rearrange("p j (u v) -> p u j v", v=4),
+                out=go_grouped[:, c, tile_cols(i), :].rearrange("p (u v) j -> p u j v", v=4),
+                in_=go_raw[:, c, :, tile_cols(i)].rearrange("p j (u v) -> p u j v", v=4),
             )
 
-        acc = [psum.tile([P, FB], F32, name="acc%d" % i) for i in range(H_TILES)]
-        for c in range(PASSES):
-            for i in range(1, H_TILES):
-                regroup(nc.scalar.copy, c, i)
-            nc.vector.tensor_tensor(
-                out=g_grouped[:, c, 0:AB, :].rearrange("p f (a e) -> p f a e", e=2),
-                in0=atom_rows[c][:].unsqueeze(2).to_broadcast([P, AB, 2, 2]),
-                in1=adj_t[:, c, :].rearrange("p (a e) -> p a e", e=2).unsqueeze(1).to_broadcast([P, AB, 2, 2]),
-                op=mybir.AluOpType.mult,
-            )
-            regroup(nc.vector.tensor_copy, c, 0)
+        def quantise_g(c):
             for lo, hi in ((0, 256), (256, DISTINCT)):
                 nc.vector.quantize_mx(
                     out=g_codes[:, c, lo:hi].bitcast(E4M3_X4),
                     scales=g_scales[:, c, lo:hi],
                     in_=g_grouped[:, c, lo:hi, :].rearrange("p f j -> p (f j)"),
                 )
+
+        def multiply(c):
             for i in range(H_TILES):
-                cols = slice(i * P, (i + 1) * P)
                 nc.vector.quantize_mx(
-                    out=go_codes[:, c, cols].bitcast(E5M2_X4),
-                    scales=go_scales[:, c, cols],
-                    in_=go_grouped[:, c, cols, :].rearrange("p h j -> p (h j)"),
+                    out=go_codes[:, c, tile_cols(i)].bitcast(E5M2_X4),
+                    scales=go_scales[:, c, tile_cols(i)],
+                    in_=go_grouped[:, c, tile_cols(i), :].rearrange("p h j -> p (h j)"),
                 )
                 nc.tensor.matmul_mx(
                     out=acc[i][:],
-                    lhsT=go_codes[:, c, cols].bitcast(E5M2_X4),
-                    lhsT_scale=go_scales[:, c, cols],
+                    lhsT=go_codes[:, c, tile_cols(i)].bitcast(E5M2_X4),
+                    lhsT_scale=go_scales[:, c, tile_cols(i)],
                     rhs=g_codes[:, c, :].bitcast(E4M3_X4),
                     rhs_scale=g_scales[:, c, :],
                     start=(c == 0),
                     stop=(c == PASSES - 1),
                 )
+
+        for c in range(PASSES):
+            for half in range(2):
+                spread_atoms(c, half)
+
+        nc.gpsimd.tensor_tensor(
+            out=g_grouped[:, :, AB:DISTINCT, :],
+            in0=bonds_t[:].rearrange("p c j e -> p c e j"),
+            in1=adj_t[:].unsqueeze(2).to_broadcast([P, PASSES, BB, PACK]),
+            op=MULT,
+        )
+        nc.gpsimd.tensor_scalar(
+            out=go_grouped[:, 0, tile_cols(HELPED), :],
+            in0=go_raw[:, 0, :, tile_cols(HELPED)].rearrange("p j h -> p h j"),
+            scalar1=1.0,
+            scalar2=0.0,
+            op0=MULT,
+            op1=ADD,
+        )
+
+        for i in range(HELPED):
+            regroup(nc.scalar.copy, 0, i)
+        gate_atoms(0, 0)
+        gate_atoms(0, 1)
+        gate_atoms(1, 0)
+        quantise_g(0)
+        multiply(0)
+
+        for i in range(HELPED):
+            regroup(nc.scalar.copy, 1, i)
+        gate_atoms(1, 1)
+        regroup(nc.vector.tensor_copy, 1, HELPED)
+        quantise_g(1)
+        multiply(1)
 
         for i in range(H_TILES):
             copy = nc.scalar.copy if i % 2 == 0 else nc.vector.tensor_copy

@@ -72,10 +72,11 @@ def tile_mpnencoder_pa_s_kernel(tc, f_atoms, f_bonds, adj, W_i_w, grad_out, out)
             ),
         )
         go_rows = grad_out.rearrange("b m n h -> (b m n) h").rearrange(
-            "(c p j) h -> c p (j h)", c=PASSES, p=P, j=PACK
+            "(c p j) h -> c p j h", c=PASSES, p=P, j=PACK
         )
         for c in range(PASSES):
-            nc.sync.dma_start(out=go_raw[:, c].rearrange("p j h -> p (j h)"), in_=go_rows[c])
+            for cols in (slice(0, H // 2), slice(H // 2, H)):
+                nc.sync.dma_start(out=go_raw[:, c, :, cols], in_=go_rows[c][:, :, cols])
 
         make_identity(nc, ident[:])
         nc.vector.memset(atoms[32:64, :], 0.0)

@@ -25,6 +25,8 @@ ROWS_PER_ATOM = P // ATOMS_PER_PASS
 
 AB = 352
 HALF = AB // 2
+PASS0_CHUNKS = ((0, 64), (64, HALF), (HALF, AB))
+PASS1_CHUNKS = ((0, HALF), (HALF, AB))
 REPEATED = 96
 BB = 32
 DISTINCT = AB + BB
@@ -88,96 +90,77 @@ def tile_mpnencoder_pa_s_kernel(tc, f_atoms, f_bonds, adj, W_i_w, grad_out, out)
         nc.vector.memset(g_codes[:, :, DISTINCT:FB].bitcast(I32), 0)
         nc.vector.memset(g_scales[:, :, DISTINCT:FB].bitcast(I32), 0)
 
-        def halves(half):
-            return slice(half * HALF, (half + 1) * HALF)
-
-        def spread_atoms(c, half):
+        def spread_atoms(c, lo, hi):
             nc.tensor.matmul(
-                out=atom_rows[c][:, halves(half), :].rearrange("p f e -> p (f e)"),
+                out=atom_rows[c][:, lo:hi, :].rearrange("p f e -> p (f e)"),
                 lhsT=spread[:, c * ATOMS_PER_PASS : (c + 1) * ATOMS_PER_PASS, :].rearrange("k m r -> k (m r)"),
-                rhs=atoms[:, halves(half)].unsqueeze(2).to_broadcast([P, HALF, 2]),
+                rhs=atoms[:, lo:hi].unsqueeze(2).to_broadcast([P, hi - lo, 2]),
                 start=True,
                 stop=True,
             )
 
-        def gate_atoms(c, half):
+        def gate_atoms(c, lo, hi):
             nc.vector.tensor_tensor(
-                out=g_grouped[:, c, halves(half), :].rearrange("p f (a e) -> p f a e", e=2),
-                in0=atom_rows[c][:, halves(half), :].unsqueeze(2).to_broadcast([P, HALF, 2, 2]),
-                in1=adj_t[:, c, :].rearrange("p (a e) -> p a e", e=2).unsqueeze(1).to_broadcast([P, HALF, 2, 2]),
+                out=g_grouped[:, c, lo:hi, :].rearrange("p f (a e) -> p f a e", e=2),
+                in0=atom_rows[c][:, lo:hi, :].unsqueeze(2).to_broadcast([P, hi - lo, 2, 2]),
+                in1=adj_t[:, c, :].rearrange("p (a e) -> p a e", e=2).unsqueeze(1).to_broadcast([P, hi - lo, 2, 2]),
                 op=MULT,
             )
 
-        def tile_cols(i):
-            return slice(i * P, (i + 1) * P)
+        def gate_bonds():
+            nc.gpsimd.tensor_tensor(
+                out=g_grouped[:, :, AB:DISTINCT, :],
+                in0=bonds_t[:].rearrange("p c j e -> p c e j"),
+                in1=adj_t[:].unsqueeze(2).to_broadcast([P, PASSES, BB, PACK]),
+                op=MULT,
+            )
 
-        def regroup(copy, c, i):
+        def tile_cols(lo, hi):
+            return slice(lo * P, hi * P)
+
+        def regroup(copy, c, lo, hi):
             copy(
-                out=go_grouped[:, c, tile_cols(i), :].rearrange("p (u v) j -> p u j v", v=4),
-                in_=go_raw[:, c, :, tile_cols(i)].rearrange("p j (u v) -> p u j v", v=4),
+                out=go_grouped[:, c, tile_cols(lo, hi), :].rearrange("p (u v) j -> p u j v", v=4),
+                in_=go_raw[:, c, :, tile_cols(lo, hi)].rearrange("p j (u v) -> p u j v", v=4),
+            )
+
+        def regroup_on_gpsimd(c, i):
+            nc.gpsimd.tensor_scalar(
+                out=go_grouped[:, c, tile_cols(i, i + 1), :],
+                in0=go_raw[:, c, :, tile_cols(i, i + 1)].rearrange("p j h -> p h j"),
+                scalar1=1.0,
+                scalar2=0.0,
+                op0=MULT,
+                op1=ADD,
             )
 
         def quantise_g(c):
-            for lo, hi in ((0, 256), (256, DISTINCT)):
+            for lo, hi, to in ((0, 256, 0), (256, DISTINCT, 256)):
                 nc.vector.quantize_mx(
-                    out=g_codes[:, c, lo:hi].bitcast(E4M3_X4),
-                    scales=g_scales[:, c, lo:hi],
+                    out=g_codes[:, c, to : to + hi - lo].bitcast(E4M3_X4),
+                    scales=g_scales[:, c, to : to + hi - lo],
                     in_=g_grouped[:, c, lo:hi, :].rearrange("p f j -> p (f j)"),
                 )
 
-        def multiply(c):
-            for i in range(H_TILES):
-                nc.vector.quantize_mx(
-                    out=go_codes[:, c, tile_cols(i)].bitcast(E5M2_X4),
-                    scales=go_scales[:, c, tile_cols(i)],
-                    in_=go_grouped[:, c, tile_cols(i), :].rearrange("p h j -> p (h j)"),
-                )
-                nc.tensor.matmul_mx(
-                    out=acc[i][:],
-                    lhsT=go_codes[:, c, tile_cols(i)].bitcast(E5M2_X4),
-                    lhsT_scale=go_scales[:, c, tile_cols(i)],
-                    rhs=g_codes[:, c, :].bitcast(E4M3_X4),
-                    rhs_scale=g_scales[:, c, :],
-                    start=(c == 0),
-                    stop=(c == PASSES - 1),
-                )
+        def quantise_go(c, lo, hi):
+            nc.vector.quantize_mx(
+                out=go_codes[:, c, tile_cols(lo, hi)].bitcast(E5M2_X4),
+                scales=go_scales[:, c, tile_cols(lo, hi)],
+                in_=go_grouped[:, c, tile_cols(lo, hi), :].rearrange("p h j -> p (h j)"),
+            )
 
-        for c in range(PASSES):
-            for half in range(2):
-                spread_atoms(c, half)
+        def multiply(c, i):
+            nc.tensor.matmul_mx(
+                out=acc[i][:],
+                lhsT=go_codes[:, c, tile_cols(i, i + 1)].bitcast(E5M2_X4),
+                lhsT_scale=go_scales[:, c, tile_cols(i, i + 1)],
+                rhs=g_codes[:, c, :].bitcast(E4M3_X4),
+                rhs_scale=g_scales[:, c, :],
+                start=(c == 0),
+                stop=(c == PASSES - 1),
+            )
 
-        nc.gpsimd.tensor_tensor(
-            out=g_grouped[:, :, AB:DISTINCT, :],
-            in0=bonds_t[:].rearrange("p c j e -> p c e j"),
-            in1=adj_t[:].unsqueeze(2).to_broadcast([P, PASSES, BB, PACK]),
-            op=MULT,
-        )
-        nc.gpsimd.tensor_scalar(
-            out=go_grouped[:, 0, tile_cols(HELPED), :],
-            in0=go_raw[:, 0, :, tile_cols(HELPED)].rearrange("p j h -> p h j"),
-            scalar1=1.0,
-            scalar2=0.0,
-            op0=MULT,
-            op1=ADD,
-        )
-
-        for i in range(HELPED):
-            regroup(nc.scalar.copy, 0, i)
-        gate_atoms(0, 0)
-        gate_atoms(0, 1)
-        gate_atoms(1, 0)
-        quantise_g(0)
-        multiply(0)
-
-        for i in range(HELPED):
-            regroup(nc.scalar.copy, 1, i)
-        gate_atoms(1, 1)
-        regroup(nc.vector.tensor_copy, 1, HELPED)
-        quantise_g(1)
-        multiply(1)
-
-        for i in range(H_TILES):
-            copy = nc.scalar.copy if i % 2 == 0 else nc.vector.tensor_copy
+        def leave(copy, i):
             copy(out=result[:, i, 0:AB], in_=acc[i][:, 0:AB])
             copy(out=result[:, i, AB : AB + REPEATED], in_=acc[i][:, AB - REPEATED : AB])
             copy(
@@ -185,3 +168,35 @@ def tile_mpnencoder_pa_s_kernel(tc, f_atoms, f_bonds, adj, W_i_w, grad_out, out)
                 in_=acc[i][:, AB:DISTINCT].unsqueeze(1).to_broadcast([P, 2, BB]),
             )
             nc.sync.dma_start(out=out[i * P : (i + 1) * P, :], in_=result[:, i, :])
+
+        on_scalar = nc.scalar.copy
+        on_vector = nc.vector.tensor_copy
+
+        for lo, hi in PASS0_CHUNKS:
+            spread_atoms(0, lo, hi)
+        for lo, hi in PASS1_CHUNKS:
+            spread_atoms(1, lo, hi)
+        gate_bonds()
+        regroup_on_gpsimd(0, 1)
+        for i in (0, 2, 3):
+            regroup(on_scalar, 0, i, i + 1)
+        for lo, hi in PASS0_CHUNKS:
+            gate_atoms(0, lo, hi)
+        gate_atoms(1, 0, HALF)
+        quantise_g(0)
+        for i in (0, 1):
+            quantise_go(0, i, i + 1)
+            multiply(0, i)
+        gate_atoms(1, HALF, AB)
+        for i in (2, 3):
+            quantise_go(0, i, i + 1)
+            multiply(0, i)
+        for i in range(3):
+            regroup(on_scalar, 1, i, i + 1)
+        regroup(on_vector, 1, 3, 4)
+        quantise_g(1)
+        for i in range(H_TILES):
+            quantise_go(1, i, i + 1)
+            multiply(1, i)
+        for i in range(H_TILES):
+            leave(on_scalar if i % 2 == 0 else on_vector, i)

@@ -25,15 +25,13 @@ ROWS_PER_ATOM = P // ATOMS_PER_PASS
 
 AB = 352
 HALF = AB // 2
-PASS0_CHUNKS = ((0, 64), (64, HALF), (HALF, AB))
-PASS1_CHUNKS = ((0, HALF), (HALF, AB))
+SPANS = ((0, 0, 64, 0), (0, 64, 208, 1), (0, 208, AB, 2), (1, 0, HALF, 0), (1, HALF, AB, 3))
 REPEATED = 96
 BB = 32
 DISTINCT = AB + BB
 FB = AB + REPEATED + BB + BB
 H = 512
 H_TILES = H // P
-HELPED = H_TILES - 1
 
 FLOPS = 2 * TOKENS * H * FB
 BYTES = 2 * (TOKENS * H + ATOMS * AB + TOKENS * BB + TOKENS) + 4 * H * FB
@@ -59,7 +57,7 @@ def tile_mpnencoder_pa_s_kernel(tc, f_atoms, f_bonds, adj, W_i_w, grad_out, out)
         g_codes = keep.tile([P, PASSES, FB], U32, align_bytes=64)
         g_scales = keep.tile([P, PASSES, FB], U8, align_bytes=64)
         result = keep.tile([P, H_TILES, FB], F32)
-        atom_rows = [psum.tile([P, AB, 2], BF16, name="atom_rows%d" % c) for c in range(PASSES)]
+        atom_rows = [psum.tile([P, HALF, 2], BF16, name="atom_rows%d" % b) for b in range(4)]
         acc = [psum.tile([P, FB], F32, name="acc%d" % i) for i in range(H_TILES)]
 
         nc.sync.dma_start(out=atoms[0:ATOMS, :], in_=f_atoms.rearrange("b m f -> (b m) f"))
@@ -76,8 +74,8 @@ def tile_mpnencoder_pa_s_kernel(tc, f_atoms, f_bonds, adj, W_i_w, grad_out, out)
         go_rows = grad_out.rearrange("b m n h -> (b m n) h").rearrange(
             "(c p j) h -> c p j h", c=PASSES, p=P, j=PACK
         )
-        for c in range(PASSES):
-            for cols in (slice(0, H // 2), slice(H // 2, H)):
+        for cols in (slice(0, H // 2), slice(H // 2, H)):
+            for c in range(PASSES):
                 nc.sync.dma_start(out=go_raw[:, c, :, cols], in_=go_rows[c][:, :, cols])
 
         make_identity(nc, ident[:])
@@ -90,19 +88,19 @@ def tile_mpnencoder_pa_s_kernel(tc, f_atoms, f_bonds, adj, W_i_w, grad_out, out)
         nc.vector.memset(g_codes[:, :, DISTINCT:FB].bitcast(I32), 0)
         nc.vector.memset(g_scales[:, :, DISTINCT:FB].bitcast(I32), 0)
 
-        def spread_atoms(c, lo, hi):
+        def spread_atoms(c, lo, hi, bank):
             nc.tensor.matmul(
-                out=atom_rows[c][:, lo:hi, :].rearrange("p f e -> p (f e)"),
+                out=atom_rows[bank][:, 0 : hi - lo, :].rearrange("p f e -> p (f e)"),
                 lhsT=spread[:, c * ATOMS_PER_PASS : (c + 1) * ATOMS_PER_PASS, :].rearrange("k m r -> k (m r)"),
                 rhs=atoms[:, lo:hi].unsqueeze(2).to_broadcast([P, hi - lo, 2]),
                 start=True,
                 stop=True,
             )
 
-        def gate_atoms(c, lo, hi):
+        def gate_atoms(c, lo, hi, bank):
             nc.vector.tensor_tensor(
                 out=g_grouped[:, c, lo:hi, :].rearrange("p f (a e) -> p f a e", e=2),
-                in0=atom_rows[c][:, lo:hi, :].unsqueeze(2).to_broadcast([P, hi - lo, 2, 2]),
+                in0=atom_rows[bank][:, 0 : hi - lo, :].unsqueeze(2).to_broadcast([P, hi - lo, 2, 2]),
                 in1=adj_t[:, c, :].rearrange("p (a e) -> p a e", e=2).unsqueeze(1).to_broadcast([P, hi - lo, 2, 2]),
                 op=MULT,
             )
@@ -172,31 +170,35 @@ def tile_mpnencoder_pa_s_kernel(tc, f_atoms, f_bonds, adj, W_i_w, grad_out, out)
         on_scalar = nc.scalar.copy
         on_vector = nc.vector.tensor_copy
 
-        for lo, hi in PASS0_CHUNKS:
-            spread_atoms(0, lo, hi)
-        for lo, hi in PASS1_CHUNKS:
-            spread_atoms(1, lo, hi)
+        for span in SPANS[:3]:
+            spread_atoms(*span)
+        gate_atoms(*SPANS[0])
+        for span in SPANS[3:]:
+            spread_atoms(*span)
         gate_bonds()
         regroup_on_gpsimd(0, 1)
-        for i in (0, 2, 3):
-            regroup(on_scalar, 0, i, i + 1)
-        for lo, hi in PASS0_CHUNKS:
-            gate_atoms(0, lo, hi)
-        gate_atoms(1, 0, HALF)
+        for c, i in ((0, 0), (1, 0), (1, 1), (0, 2), (1, 2), (0, 3)):
+            regroup(on_scalar, c, i, i + 1)
+
+        def contract(c, i):
+            quantise_go(c, i, i + 1)
+            multiply(c, i)
+
+        for span in SPANS[1:4]:
+            gate_atoms(*span)
         quantise_g(0)
-        for i in (0, 1):
-            quantise_go(0, i, i + 1)
-            multiply(0, i)
-        gate_atoms(1, HALF, AB)
-        for i in (2, 3):
-            quantise_go(0, i, i + 1)
-            multiply(0, i)
-        for i in range(3):
-            regroup(on_scalar, 1, i, i + 1)
-        regroup(on_vector, 1, 3, 4)
+        contract(0, 0)
+        gate_atoms(*SPANS[4])
+        contract(0, 1)
         quantise_g(1)
-        for i in range(H_TILES):
-            quantise_go(1, i, i + 1)
-            multiply(1, i)
-        for i in range(H_TILES):
-            leave(on_scalar if i % 2 == 0 else on_vector, i)
+        contract(1, 0)
+        contract(1, 1)
+        regroup(on_vector, 1, 3, 4)
+        contract(0, 2)
+        contract(1, 2)
+        contract(0, 3)
+        contract(1, 3)
+        leave(on_scalar, 0)
+        leave(on_scalar, 1)
+        leave(on_vector, 2)
+        leave(on_scalar, 3)

@@ -27,6 +27,7 @@ AB = 352
 HALF = AB // 2
 SPANS = ((0, 0, 64, 0), (0, 64, 208, 1), (0, 208, AB, 2), (1, 0, HALF, 0), (1, HALF, AB, 3))
 REPEATED = 96
+SINGLE = AB - REPEATED
 BB = 32
 DISTINCT = AB + BB
 FB = AB + REPEATED + BB + BB
@@ -50,9 +51,9 @@ def tile_mpnencoder_pa_s_kernel(tc, f_atoms, f_bonds, adj, W_i_w, grad_out, out)
         adj_t = keep.tile([P, PASSES, PACK], BF16)
         bonds_t = keep.tile([P, PASSES, PACK, BB], BF16)
         go_raw = keep.tile([P, PASSES, PACK, H], BF16)
-        go_grouped = keep.tile([P, PASSES, H, PACK], BF16, align_bytes=64)
-        go_codes = keep.tile([P, PASSES, H], U32, align_bytes=64)
-        go_scales = keep.tile([P, PASSES, H], U8, align_bytes=64)
+        go_grouped = keep.tile([P, H_TILES, PASSES, P, PACK], BF16, align_bytes=64)
+        go_codes = keep.tile([P, H_TILES, PASSES, P], U32, align_bytes=64)
+        go_scales = keep.tile([P, H_TILES, PASSES, P], U8, align_bytes=64)
         g_grouped = keep.tile([P, PASSES, DISTINCT, PACK], BF16, align_bytes=64)
         g_codes = keep.tile([P, PASSES, FB], U32, align_bytes=64)
         g_scales = keep.tile([P, PASSES, FB], U8, align_bytes=64)
@@ -113,19 +114,19 @@ def tile_mpnencoder_pa_s_kernel(tc, f_atoms, f_bonds, adj, W_i_w, grad_out, out)
                 op=MULT,
             )
 
-        def tile_cols(lo, hi):
-            return slice(lo * P, hi * P)
+        def tile_cols(i):
+            return slice(i * P, (i + 1) * P)
 
-        def regroup(copy, c, lo, hi):
+        def regroup(copy, c, i):
             copy(
-                out=go_grouped[:, c, tile_cols(lo, hi), :].rearrange("p (u v) j -> p u j v", v=4),
-                in_=go_raw[:, c, :, tile_cols(lo, hi)].rearrange("p j (u v) -> p u j v", v=4),
+                out=go_grouped[:, i, c, :, :].rearrange("p (u v) j -> p u j v", v=4),
+                in_=go_raw[:, c, :, tile_cols(i)].rearrange("p j (u v) -> p u j v", v=4),
             )
 
         def regroup_on_gpsimd(c, i):
             nc.gpsimd.tensor_scalar(
-                out=go_grouped[:, c, tile_cols(i, i + 1), :],
-                in0=go_raw[:, c, :, tile_cols(i, i + 1)].rearrange("p j h -> p h j"),
+                out=go_grouped[:, i, c, :, :],
+                in0=go_raw[:, c, :, tile_cols(i)].rearrange("p j h -> p h j"),
                 scalar1=1.0,
                 scalar2=0.0,
                 op0=MULT,
@@ -140,32 +141,40 @@ def tile_mpnencoder_pa_s_kernel(tc, f_atoms, f_bonds, adj, W_i_w, grad_out, out)
                     in_=g_grouped[:, c, lo:hi, :].rearrange("p f j -> p (f j)"),
                 )
 
-        def quantise_go(c, lo, hi):
+        def quantise_go(i, first, end):
             nc.vector.quantize_mx(
-                out=go_codes[:, c, tile_cols(lo, hi)].bitcast(E5M2_X4),
-                scales=go_scales[:, c, tile_cols(lo, hi)],
-                in_=go_grouped[:, c, tile_cols(lo, hi), :].rearrange("p h j -> p (h j)"),
+                out=go_codes[:, i, first:end, :].rearrange("p c h -> p (c h)").bitcast(E5M2_X4),
+                scales=go_scales[:, i, first:end, :].rearrange("p c h -> p (c h)"),
+                in_=go_grouped[:, i, first:end, :, :].rearrange("p c h j -> p (c h j)"),
             )
 
         def multiply(c, i):
             nc.tensor.matmul_mx(
                 out=acc[i][:],
-                lhsT=go_codes[:, c, tile_cols(i, i + 1)].bitcast(E5M2_X4),
-                lhsT_scale=go_scales[:, c, tile_cols(i, i + 1)],
+                lhsT=go_codes[:, i, c, :].bitcast(E5M2_X4),
+                lhsT_scale=go_scales[:, i, c, :],
                 rhs=g_codes[:, c, :].bitcast(E4M3_X4),
                 rhs_scale=g_scales[:, c, :],
                 start=(c == 0),
                 stop=(c == PASSES - 1),
             )
 
-        def leave(copy, i):
-            copy(out=result[:, i, 0:AB], in_=acc[i][:, 0:AB])
-            copy(out=result[:, i, AB : AB + REPEATED], in_=acc[i][:, AB - REPEATED : AB])
+        def store(i, lo, hi):
+            nc.sync.dma_start(out=out[i * P : (i + 1) * P, lo:hi], in_=result[:, i, lo:hi])
+
+        def leave(copy, i, halves=False):
+            copy(out=result[:, i, 0:SINGLE], in_=acc[i][:, 0:SINGLE])
+            if halves:
+                store(i, 0, SINGLE)
+            copy(
+                out=result[:, i, SINGLE : AB + REPEATED].rearrange("p (r f) -> p r f", r=2),
+                in_=acc[i][:, SINGLE:AB].unsqueeze(1).to_broadcast([P, 2, REPEATED]),
+            )
             copy(
                 out=result[:, i, AB + REPEATED : FB].rearrange("p (r e) -> p r e", r=2),
                 in_=acc[i][:, AB:DISTINCT].unsqueeze(1).to_broadcast([P, 2, BB]),
             )
-            nc.sync.dma_start(out=out[i * P : (i + 1) * P, :], in_=result[:, i, :])
+            store(i, SINGLE if halves else 0, FB)
 
         on_scalar = nc.scalar.copy
         on_vector = nc.vector.tensor_copy
@@ -178,27 +187,27 @@ def tile_mpnencoder_pa_s_kernel(tc, f_atoms, f_bonds, adj, W_i_w, grad_out, out)
         gate_bonds()
         regroup_on_gpsimd(0, 1)
         for c, i in ((0, 0), (1, 0), (1, 1), (0, 2), (1, 2), (0, 3)):
-            regroup(on_scalar, c, i, i + 1)
+            regroup(on_scalar, c, i)
 
-        def contract(c, i):
-            quantise_go(c, i, i + 1)
-            multiply(c, i)
+        def contract(i, first, end):
+            quantise_go(i, first, end)
+            for c in range(first, end):
+                multiply(c, i)
 
         for span in SPANS[1:4]:
             gate_atoms(*span)
         quantise_g(0)
-        contract(0, 0)
+        contract(0, 0, 1)
         gate_atoms(*SPANS[4])
-        contract(0, 1)
+        contract(1, 0, 1)
         quantise_g(1)
-        contract(1, 0)
-        contract(1, 1)
-        regroup(on_vector, 1, 3, 4)
-        contract(0, 2)
-        contract(1, 2)
-        contract(0, 3)
-        contract(1, 3)
-        leave(on_scalar, 0)
-        leave(on_scalar, 1)
+        contract(0, 1, 2)
+        contract(1, 1, 2)
+        contract(2, 0, 2)
+        regroup(on_vector, 1, 3)
+        contract(3, 0, 1)
+        contract(3, 1, 2)
+        leave(on_scalar, 0, halves=True)
+        leave(on_scalar, 1, halves=True)
         leave(on_vector, 2)
-        leave(on_scalar, 3)
+        leave(on_scalar, 3, halves=True)

@@ -33,6 +33,7 @@ DISTINCT = AB + BB
 FB = AB + REPEATED + BB + BB
 H = 512
 H_TILES = H // P
+RUN = 8
 
 FLOPS = 2 * TOKENS * H * FB
 BYTES = 2 * (TOKENS * H + ATOMS * AB + TOKENS * BB + TOKENS) + 4 * H * FB
@@ -119,8 +120,8 @@ def tile_mpnencoder_pa_s_kernel(tc, f_atoms, f_bonds, adj, W_i_w, grad_out, out)
 
         def regroup(copy, c, i):
             copy(
-                out=go_grouped[:, i, c, :, :].rearrange("p (u v) j -> p u j v", v=4),
-                in_=go_raw[:, c, :, tile_cols(i)].rearrange("p j (u v) -> p u j v", v=4),
+                out=go_grouped[:, i, c, :, :].rearrange("p (u v) j -> p u j v", v=RUN),
+                in_=go_raw[:, c, :, tile_cols(i)].rearrange("p j (u v) -> p u j v", v=RUN),
             )
 
         def regroup_on_gpsimd(c, i):

from contextlib import ExitStack

import concourse.mybir as mybir
from concourse.masks import make_identity

BF16 = mybir.dt.bfloat16
F32 = mybir.dt.float32
I32 = mybir.dt.int32
U32 = mybir.dt.uint32
U8 = mybir.dt.uint8
E4M3_X4 = mybir.dt.float8_e4m3fn_x4
E5M2_X4 = mybir.dt.float8_e5m2_x4
MULT = mybir.AluOpType.mult
ADD = mybir.AluOpType.add

P = 128
PACK = 4
K_PASS = P * PACK

ATOMS = 32
TOKENS = ATOMS * ATOMS
PASSES = TOKENS // K_PASS
ATOMS_PER_PASS = ATOMS // PASSES
ROWS_PER_ATOM = P // ATOMS_PER_PASS

AB = 352
HALF = AB // 2
SPANS = ((0, 0, 64, 0), (0, 64, 208, 1), (0, 208, AB, 2), (1, 0, HALF, 0), (1, HALF, AB, 3))
REPEATED = 96
SINGLE = AB - REPEATED
BB = 32
DISTINCT = AB + BB
FB = AB + REPEATED + BB + BB
H = 512
H_TILES = H // P
RUN = 8

FLOPS = 2 * TOKENS * H * FB
BYTES = 2 * (TOKENS * H + ATOMS * AB + TOKENS * BB + TOKENS) + 4 * H * FB


def tile_mpnencoder_pa_s_kernel(tc, f_atoms, f_bonds, adj, W_i_w, grad_out, out):
    nc = tc.nc
    with ExitStack() as ctx:
        keep = ctx.enter_context(tc.tile_pool(name="keep", bufs=1))
        psum = ctx.enter_context(tc.psum_pool(name="psum", bufs=1))
        ctx.enter_context(tc.manual_schedule())

        ident = keep.tile([P, P], BF16)
        spread = keep.tile([P, ATOMS, ROWS_PER_ATOM], BF16)
        atoms = keep.tile([P, AB], BF16)
        adj_t = keep.tile([P, PASSES, PACK], BF16)
        bonds_t = keep.tile([P, PASSES, PACK, BB], BF16)
        go_raw = keep.tile([P, PASSES, PACK, H], BF16)
        go_grouped = keep.tile([P, H_TILES, PASSES, P, PACK], BF16, align_bytes=64)
        go_codes = keep.tile([P, H_TILES, PASSES, P], U32, align_bytes=64)
        go_scales = keep.tile([P, H_TILES, PASSES, P], U8, align_bytes=64)
        g_grouped = keep.tile([P, PASSES, DISTINCT, PACK], BF16, align_bytes=64)
        g_codes = keep.tile([P, PASSES, FB], U32, align_bytes=64)
        g_scales = keep.tile([P, PASSES, FB], U8, align_bytes=64)
        result = keep.tile([P, H_TILES, FB], F32)
        atom_rows = [psum.tile([P, HALF, 2], BF16, name="atom_rows%d" % b) for b in range(4)]
        acc = [psum.tile([P, FB], F32, name="acc%d" % i) for i in range(H_TILES)]

        nc.sync.dma_start(out=atoms[0:ATOMS, :], in_=f_atoms.rearrange("b m f -> (b m) f"))
        nc.sync.dma_start(
            out=adj_t[:],
            in_=adj.rearrange("b m n -> (b m n)").rearrange("(c p j) -> p c j", c=PASSES, p=P, j=PACK),
        )
        nc.sync.dma_start(
            out=bonds_t[:].rearrange("p c j e -> p c (j e)"),
            in_=f_bonds.rearrange("b m n e -> (b m n) e").rearrange(
                "(c p j) e -> p c (j e)", c=PASSES, p=P, j=PACK
            ),
        )
        go_rows = grad_out.rearrange("b m n h -> (b m n) h").rearrange(
            "(c p j) h -> c p j h", c=PASSES, p=P, j=PACK
        )
        for cols in (slice(0, H // 2), slice(H // 2, H)):
            for c in range(PASSES):
                nc.sync.dma_start(out=go_raw[:, c, :, cols], in_=go_rows[c][:, :, cols])

        make_identity(nc, ident[:])
        nc.vector.memset(atoms[32:64, :], 0.0)
        nc.vector.memset(atoms[64:128, :], 0.0)
        nc.vector.tensor_copy(
            out=spread[:],
            in_=ident[:, 0:ATOMS].unsqueeze(2).to_broadcast([P, ATOMS, ROWS_PER_ATOM]),
        )
        nc.vector.memset(g_codes[:, :, DISTINCT:FB].bitcast(I32), 0)
        nc.vector.memset(g_scales[:, :, DISTINCT:FB].bitcast(I32), 0)

        def spread_atoms(c, lo, hi, bank):
            nc.tensor.matmul(
                out=atom_rows[bank][:, 0 : hi - lo, :].rearrange("p f e -> p (f e)"),
                lhsT=spread[:, c * ATOMS_PER_PASS : (c + 1) * ATOMS_PER_PASS, :].rearrange("k m r -> k (m r)"),
                rhs=atoms[:, lo:hi].unsqueeze(2).to_broadcast([P, hi - lo, 2]),
                start=True,
                stop=True,
            )

        def gate_atoms(c, lo, hi, bank):
            nc.vector.tensor_tensor(
                out=g_grouped[:, c, lo:hi, :].rearrange("p f (a e) -> p f a e", e=2),
                in0=atom_rows[bank][:, 0 : hi - lo, :].unsqueeze(2).to_broadcast([P, hi - lo, 2, 2]),
                in1=adj_t[:, c, :].rearrange("p (a e) -> p a e", e=2).unsqueeze(1).to_broadcast([P, hi - lo, 2, 2]),
                op=MULT,
            )

        def gate_bonds():
            nc.gpsimd.tensor_tensor(
                out=g_grouped[:, :, AB:DISTINCT, :],
                in0=bonds_t[:].rearrange("p c j e -> p c e j"),
                in1=adj_t[:].unsqueeze(2).to_broadcast([P, PASSES, BB, PACK]),
                op=MULT,
            )

        def tile_cols(i):
            return slice(i * P, (i + 1) * P)

        def regroup(copy, c, i):
            copy(
                out=go_grouped[:, i, c, :, :].rearrange("p (u v) j -> p u j v", v=RUN),
                in_=go_raw[:, c, :, tile_cols(i)].rearrange("p j (u v) -> p u j v", v=RUN),
            )

        def regroup_on_gpsimd(c, i):
            nc.gpsimd.tensor_scalar(
                out=go_grouped[:, i, c, :, :],
                in0=go_raw[:, c, :, tile_cols(i)].rearrange("p j h -> p h j"),
                scalar1=1.0,
                scalar2=0.0,
                op0=MULT,
                op1=ADD,
            )

        def quantise_g(c):
            for lo, hi, to in ((0, 256, 0), (256, DISTINCT, 256)):
                nc.vector.quantize_mx(
                    out=g_codes[:, c, to : to + hi - lo].bitcast(E4M3_X4),
                    scales=g_scales[:, c, to : to + hi - lo],
                    in_=g_grouped[:, c, lo:hi, :].rearrange("p f j -> p (f j)"),
                )

        def quantise_go(i, first, end):
            nc.vector.quantize_mx(
                out=go_codes[:, i, first:end, :].rearrange("p c h -> p (c h)").bitcast(E5M2_X4),
                scales=go_scales[:, i, first:end, :].rearrange("p c h -> p (c h)"),
                in_=go_grouped[:, i, first:end, :, :].rearrange("p c h j -> p (c h j)"),
            )

        def multiply(c, i):
            nc.tensor.matmul_mx(
                out=acc[i][:],
                lhsT=go_codes[:, i, c, :].bitcast(E5M2_X4),
                lhsT_scale=go_scales[:, i, c, :],
                rhs=g_codes[:, c, :].bitcast(E4M3_X4),
                rhs_scale=g_scales[:, c, :],
                start=(c == 0),
                stop=(c == PASSES - 1),
            )

        def store(i, lo, hi):
            nc.sync.dma_start(out=out[i * P : (i + 1) * P, lo:hi], in_=result[:, i, lo:hi])

        def leave(copy, i, halves=False):
            copy(out=result[:, i, 0:SINGLE], in_=acc[i][:, 0:SINGLE])
            if halves:
                store(i, 0, SINGLE)
            copy(
                out=result[:, i, SINGLE : AB + REPEATED].rearrange("p (r f) -> p r f", r=2),
                in_=acc[i][:, SINGLE:AB].unsqueeze(1).to_broadcast([P, 2, REPEATED]),
            )
            copy(
                out=result[:, i, AB + REPEATED : FB].rearrange("p (r e) -> p r e", r=2),
                in_=acc[i][:, AB:DISTINCT].unsqueeze(1).to_broadcast([P, 2, BB]),
            )
            store(i, SINGLE if halves else 0, FB)

        on_scalar = nc.scalar.copy
        on_vector = nc.vector.tensor_copy

        for span in SPANS[:3]:
            spread_atoms(*span)
        gate_atoms(*SPANS[0])
        for span in SPANS[3:]:
            spread_atoms(*span)
        gate_bonds()
        regroup_on_gpsimd(0, 1)
        for c, i in ((0, 0), (1, 0), (1, 1), (0, 2), (1, 2), (0, 3)):
            regroup(on_scalar, c, i)

        def contract(i, first, end):
            quantise_go(i, first, end)
            for c in range(first, end):
                multiply(c, i)

        for span in SPANS[1:4]:
            gate_atoms(*span)
        quantise_g(0)
        contract(0, 0, 1)
        gate_atoms(*SPANS[4])
        contract(1, 0, 1)
        quantise_g(1)
        contract(0, 1, 2)
        contract(1, 1, 2)
        contract(2, 0, 2)
        regroup(on_vector, 1, 3)
        contract(3, 0, 1)
        contract(3, 1, 2)
        leave(on_scalar, 0, halves=True)
        leave(on_scalar, 1, halves=True)
        leave(on_vector, 2)
        leave(on_scalar, 3, halves=True)
